import numpy as np
import ml_dtypes


def mxq(x, axis, fmt="e4m3"):
    dtype, down = {"e4m3": (ml_dtypes.float8_e4m3fn, 7), "e5m2": (ml_dtypes.float8_e5m2, 14)}[fmt]
    v = np.moveaxis(np.asarray(x, np.float32).astype(ml_dtypes.bfloat16).astype(np.float64), axis, -1)
    blocks = v.reshape(v.shape[:-1] + (-1, 32))
    amax = np.abs(blocks).max(-1, keepdims=True)
    byte = np.maximum(np.where(amax > 0, np.frexp(amax)[1] - 1 + 127, 0) - down, 1)
    scale = np.exp2(byte - 127.0)
    codes = (blocks / scale).astype(np.float32).astype(dtype).astype(np.float64)
    return np.moveaxis((codes * scale).reshape(v.shape), -1, axis)


WIDE = False


def mx_kscale(k):
    if not WIDE:
        return np.ones(k)
    levels = np.array([10, -10, 5, -5, 0])
    a = np.random.permutation(np.resize(levels, k // 512 * 4)).reshape(k // 512, 4)
    idx = np.arange(k)
    return np.exp2(a[idx // 512, idx % 128 // 32])


BF16 = ml_dtypes.bfloat16


def bf(x):
    return np.asarray(x, np.float32).astype(BF16)


def f64(x):
    return np.asarray(x).astype(np.float64)


E2M1 = np.array([0.0, 0.5, 1.0, 1.5, 2.0, 3.0, 4.0, 6.0, -0.0, -0.5, -1.0, -1.5, -2.0, -3.0, -4.0, -6.0])


def pack_weight(w, fmt):
    k, n = w.shape
    w = f64(bf(w)).reshape(k // 32, 32, n)
    amax = np.abs(w).max(1)
    if fmt == "e4m3":
        byte = np.frexp(amax)[1] - 1 + 127 - 7
    else:
        mant, ex = np.frexp(amax / 6.0)
        byte = np.where(mant > 0.5, ex, ex - 1) + 127
    byte = np.clip(np.where(amax > 0, byte, 1), 1, 254)
    scaled = (w * np.exp2(127.0 - byte)[:, None, :]).reshape(k, n).astype(np.float32)
    by_word = np.ascontiguousarray(scaled.reshape(k // 512, 128, 4, n).transpose(0, 1, 3, 2))
    if fmt == "e4m3":
        words = by_word.astype(ml_dtypes.float8_e4m3fn).view(np.uint8)
    else:
        c = by_word.astype(ml_dtypes.float4_e2m1fn).view(np.uint8) & 0xF
        words = c[..., 0::2] | (c[..., 1::2] << 4)
    return np.ascontiguousarray(words), np.ascontiguousarray(byte.astype(np.uint8).reshape(k // 512, 16, n))


def unpack_weight(words, scales, fmt):
    g, p, n, _ = words.shape
    if fmt == "e4m3":
        vals = np.ascontiguousarray(words).view(ml_dtypes.float8_e4m3fn).astype(np.float64)
    else:
        nib = np.empty((g, p, n, 4), np.uint8)
        nib[..., 0::2] = words & 0xF
        nib[..., 1::2] = words >> 4
        vals = E2M1[nib]
    vals = vals * np.repeat(np.exp2(scales.astype(np.float64) - 127.0), 8, axis=1)[..., None]
    return vals.transpose(0, 1, 3, 2).reshape(g * 512, n)

def pack4(w):
    words, scales = pack_weight(w, "e2m1")
    return words.reshape(words.shape[0], 128, -1), scales


def unpack4(words, scales):
    return unpack_weight(words.reshape(words.shape[0], 128, -1, 2), scales, "e2m1")


B, D, H, F, K = 256, 16384, 1024, 1024, 128
EPS_LN = 1e-5


def silu(v):
    return v / (1.0 + np.exp(-v))


def setup_inputs():
    s = mx_kscale(D)
    x = bf(np.random.standard_normal((B, D)) * s)
    W1_words, W1_scales = pack4(np.random.standard_normal((D, H)) / np.sqrt(D) / s[:, None])
    return {"x": x,
            "W1_words": W1_words,
            "W1_scales": W1_scales,
            "b1": bf(0.2 * np.random.standard_normal(H)),
            "g": bf(1.0 + 0.1 * np.random.standard_normal(H)),
            "beta": bf(0.1 * np.random.standard_normal(H))}


def reference(x, W1_words, W1_scales, b1, g, beta):
    h = silu((mxq(f64(x), 1, "e4m3") @ unpack4(W1_words, W1_scales)) + f64(b1))
    mu = h.mean(-1, keepdims=True)
    var = ((h - mu) ** 2).mean(-1, keepdims=True)
    return (h - mu) / np.sqrt(var + EPS_LN) * f64(g) + f64(beta)

@@ -1,0 +1,275 @@
+from contextlib import ExitStack
+
+import concourse.mybir as mybir
+from concourse.masks import make_identity
+
+F32 = mybir.dt.float32
+BF16 = mybir.dt.bfloat16
+I32 = mybir.dt.int32
+U32 = mybir.dt.uint32
+U8 = mybir.dt.uint8
+FP8X4 = mybir.dt.float8_e4m3fn_x4
+FP4X4 = mybir.dt.float4_e2m1fn_x4
+ALU = mybir.AluOpType
+ACT = mybir.ActivationFunctionType
+
+P = 128
+ROWS = 256
+K = 16384
+H = 1024
+EPS_LN = 1e-5
+
+K_PASS = 4 * P
+GROUPS = K // K_PASS
+ROW_TILES = ROWS // P
+N_PASS = 512
+COL_HALVES = H // N_PASS
+PAIRS = 2
+
+ROUND_GROUPS = 4
+BATCH_GROUPS = 8
+LOADS_AHEAD = 3
+
+FLOPS = 2 * ROWS * K * H
+
+
+def cut_rounds():
+    rounds = []
+    first = 0
+    while first < GROUPS:
+        count = min(ROUND_GROUPS, max(1, first), max(1, (GROUPS - first) // 2))
+        rounds.append((first, count))
+        first += count
+    return rounds
+
+
+def tile_evidentialhead_pa_k_kernel(tc, x, W1_words, W1_scales, b1, g, beta, out):
+    nc = tc.nc
+    rounds = cut_rounds()
+    vectors = (b1, g, beta)
+    x_by_tile = x.rearrange("(t b) k -> b t k", t=ROW_TILES)
+
+    with ExitStack() as ctx:
+        ctx.enter_context(tc.manual_schedule())
+        keep = ctx.enter_context(tc.tile_pool(name="keep", bufs=1))
+        x_pool = ctx.enter_context(tc.tile_pool(name="x_pool", bufs=LOADS_AHEAD + 1))
+        w_pool = ctx.enter_context(tc.tile_pool(name="w_pool", bufs=LOADS_AHEAD + 1))
+        stage = ctx.enter_context(tc.tile_pool(name="stage", bufs=2))
+        codes = ctx.enter_context(tc.tile_pool(name="codes", bufs=2))
+        sums_pool = ctx.enter_context(tc.psum_pool(name="sums_pool", bufs=1))
+        banks = ctx.enter_context(tc.psum_pool(name="banks", bufs=4))
+
+        w_planes_of = {}
+        for batch in range(GROUPS // BATCH_GROUPS):
+            w_planes_of[batch] = keep.tile(
+                [P, BATCH_GROUPS, H], U8, name="w_planes_%d" % batch, align_bytes=64
+            )
+        ident = keep.tile([P, P], F32)
+        ones = keep.tile([P, P], BF16)
+        vec_rows = keep.tile([P, len(vectors), H], BF16)
+        spread = keep.tile([P, len(vectors), H], F32)
+        neg_half = keep.tile([P, 1], F32)
+        acc = {}
+        for t in range(ROW_TILES):
+            for c in range(COL_HALVES):
+                acc[(t, c)] = sums_pool.tile([P, N_PASS], F32, name="acc_%d_%d" % (t, c))
+
+        def zero_planes(batch):
+            nc.vector.memset(w_planes_of[batch][:].bitcast(I32), 0)
+
+        zero_planes(0)
+        make_identity(nc, ident[:])
+        nc.gpsimd.memset(ones[:], 1.0)
+        nc.gpsimd.memset(vec_rows[:].bitcast(F32), 0.0)
+        nc.gpsimd.memset(neg_half[:], -0.5)
+        for j, vector in enumerate(vectors):
+            nc.scalar.dma_start(out=vec_rows[0:1, j, :], in_=vector.unsqueeze(0))
+
+        x_raw_of = {}
+        x_sorted_of = {}
+        grouped_of = {}
+        w_words_of = {}
+        x_codes_of = {}
+        x_planes_of = {}
+
+        def load_x(i):
+            first, count = rounds[i]
+            x_raw = x_pool.tile([P, ROW_TILES, count * K_PASS], BF16, tag="x_raw")
+            nc.sync.dma_start(
+                out=x_raw[:], in_=x_by_tile[:, :, first * K_PASS : (first + count) * K_PASS]
+            )
+            x_raw_of[i] = x_raw
+
+        def load_scales(batch):
+            groups = slice(BATCH_GROUPS * batch, BATCH_GROUPS * (batch + 1))
+            for low in range(2):
+                for r in range(4):
+                    nc.sync.dma_start(
+                        out=w_planes_of[batch][32 * low + r : P : 64, :, :].bitcast(I32),
+                        in_=W1_scales[groups, 4 * low + r : 16 : 8, :]
+                        .bitcast(I32)
+                        .rearrange("g q n -> q g n"),
+                    )
+
+        def load_w(i):
+            first, count = rounds[i]
+            if first % BATCH_GROUPS == 0:
+                load_scales(first // BATCH_GROUPS)
+            w_words = w_pool.tile([P, count, 2 * H], U8, tag="w_words", align_bytes=64)
+            nc.sync.dma_start(
+                out=w_words[:].bitcast(I32),
+                in_=W1_words[first : first + count].bitcast(I32).rearrange("g p n -> p g n"),
+            )
+            w_words_of[i] = w_words
+
+        def sort_words(i):
+            count = rounds[i][1]
+            x_sorted = stage.tile([P, ROW_TILES, count, PAIRS, P], F32, tag="x_sorted")
+            nc.vector.tensor_copy(
+                out=x_sorted[:].rearrange("b t g u p -> b (t g) u p"),
+                in_=x_raw_of[i][:]
+                .bitcast(F32)
+                .rearrange("b t (g p u) -> b (t g) u p", p=P, u=PAIRS),
+            )
+            x_sorted_of[i] = x_sorted
+
+        def turn(i):
+            count = rounds[i][1]
+            grouped = stage.tile(
+                [P, count * ROW_TILES * P * 4], BF16, tag="grouped", align_bytes=64
+            )
+            grouped_words = grouped[:].bitcast(F32).rearrange(
+                "p (g t r u) -> p g t r u", g=count, t=ROW_TILES, u=PAIRS
+            )
+            for j in range(count):
+                bank = banks.tile([P, ROW_TILES, PAIRS, P], F32, tag="bank")
+                for t in range(ROW_TILES):
+                    for u in range(PAIRS):
+                        nc.tensor.transpose(
+                            bank[:, t, u, :], x_sorted_of[i][:, t, j, u, :], ident[:]
+                        )
+                nc.scalar.copy(
+                    out=grouped_words[:, j], in_=bank[:].rearrange("p t u r -> p t r u")
+                )
+            grouped_of[i] = grouped
+
+        def quantise(i):
+            count = rounds[i][1]
+            x_codes = codes.tile([P, count, ROW_TILES, P], U32, tag="x_codes", align_bytes=64)
+            x_planes = codes.tile([P, count, ROW_TILES, P], U8, tag="x_planes", align_bytes=64)
+            nc.vector.quantize_mx(
+                out=x_codes[:].rearrange("p g t r -> p (g t r)").bitcast(FP8X4),
+                scales=x_planes[:].rearrange("p g t r -> p (g t r)"),
+                in_=grouped_of[i][:],
+            )
+            x_codes_of[i] = x_codes
+            x_planes_of[i] = x_planes
+
+        def multiply(i):
+            first, count = rounds[i]
+            for j in range(count):
+                group = first + j
+                w_planes = w_planes_of[group // BATCH_GROUPS]
+                for t in range(ROW_TILES):
+                    for c in range(COL_HALVES):
+                        nc.tensor.matmul_mx(
+                            out=acc[(t, c)][:],
+                            lhsT=x_codes_of[i][:, j, t, :].bitcast(FP8X4),
+                            lhsT_scale=x_planes_of[i][:, j, t, :],
+                            rhs=w_words_of[i][
+                                :, j, 2 * N_PASS * c : 2 * N_PASS * (c + 1)
+                            ].bitcast(FP4X4),
+                            rhs_scale=w_planes[
+                                :, group % BATCH_GROUPS, N_PASS * c : N_PASS * (c + 1)
+                            ],
+                            start=(group == 0),
+                            stop=(group == GROUPS - 1),
+                        )
+
+        def spread_vector(j):
+            for c in range(COL_HALVES):
+                cols = slice(N_PASS * c, N_PASS * (c + 1))
+                bank = banks.tile([P, N_PASS], F32, tag="bank")
+                nc.tensor.matmul(
+                    out=bank[:], lhsT=ones[:], rhs=vec_rows[:, j, cols], start=True, stop=True
+                )
+                nc.scalar.copy(out=spread[:, j, cols], in_=bank[:])
+
+        load_x(0)
+        for i in range(LOADS_AHEAD):
+            load_x(i + 1)
+            load_w(i)
+        sort_words(0)
+        turn(0)
+        for i in range(len(rounds)):
+            if i + LOADS_AHEAD + 1 < len(rounds):
+                load_x(i + LOADS_AHEAD + 1)
+            if i + LOADS_AHEAD < len(rounds):
+                load_w(i + LOADS_AHEAD)
+            if i + 1 < len(rounds):
+                sort_words(i + 1)
+            quantise(i)
+            if i + 1 < GROUPS // BATCH_GROUPS:
+                zero_planes(i + 1)
+            if i + 1 < len(rounds):
+                turn(i + 1)
+            multiply(i)
+            if i < len(vectors):
+                spread_vector(i)
+
+        h_of = {}
+        row_sums_of = {}
+        centred_of = {}
+        square_sum_of = {}
+        for t in range(ROW_TILES):
+            h = keep.tile([P, H], F32, name="h_%d" % t)
+            row_sums = keep.tile([P, COL_HALVES], F32, name="row_sums_%d" % t)
+            for c in range(COL_HALVES):
+                cols = slice(N_PASS * c, N_PASS * (c + 1))
+                nc.vector.tensor_tensor(
+                    out=h[:, cols], in0=acc[(t, c)][:], in1=spread[:, 0, cols], op=ALU.add
+                )
+                nc.scalar.activation(
+                    out=h[:, cols], in_=h[:, cols], func=ACT.Silu,
+                    accum_out=row_sums[:, c : c + 1],
+                )
+            h_of[t] = h
+            row_sums_of[t] = row_sums
+
+        for t in range(ROW_TILES):
+            neg_mean = keep.tile([P, 1], F32, name="neg_mean_%d" % t)
+            nc.gpsimd.tensor_scalar(
+                out=neg_mean[:], in0=row_sums_of[t][:, 0:1], scalar1=row_sums_of[t][:, 1:2],
+                scalar2=-1.0 / H, op0=ALU.add, op1=ALU.mult,
+            )
+            squares = keep.tile([P, H], F32, name="squares_%d" % t)
+            square_sum = keep.tile([P, 1], F32, name="square_sum_%d" % t)
+            nc.scalar.activation(
+                out=squares[:], in_=h_of[t][:], func=ACT.Square, bias=neg_mean[:, 0:1],
+                accum_out=square_sum[:, 0:1],
+            )
+            centred = keep.tile([P, H], F32, name="centred_%d" % t)
+            nc.vector.scalar_tensor_tensor(
+                out=centred[:], in0=h_of[t][:], scalar=neg_mean[:, 0:1], in1=spread[:, 1, :],
+                op0=ALU.add, op1=ALU.mult,
+            )
+            square_sum_of[t] = square_sum
+            centred_of[t] = centred
+
+        for t in range(ROW_TILES):
+            var_eps = keep.tile([P, 1], F32, name="var_eps_%d" % t)
+            nc.gpsimd.tensor_scalar(
+                out=var_eps[:], in0=square_sum_of[t][:], scalar1=1.0 / H, scalar2=EPS_LN,
+                op0=ALU.mult, op1=ALU.add,
+            )
+            rstd = keep.tile([P, 1], F32, name="rstd_%d" % t)
+            nc.gpsimd.tensor_tensor(out=rstd[:], in0=var_eps[:], in1=neg_half[:], op=ALU.pow)
+            for c in range(COL_HALVES):
+                cols = slice(N_PASS * c, N_PASS * (c + 1))
+                nc.vector.scalar_tensor_tensor(
+                    out=centred_of[t][:, cols], in0=centred_of[t][:, cols], scalar=rstd[:, 0:1],
+                    in1=spread[:, 2, cols], op0=ALU.mult, op1=ALU.add,
+                )
+                nc.sync.dma_start(
+                    out=out[P * t : P * (t + 1), cols], in_=centred_of[t][:, cols]
+                )

@@ -28,6 +28,7 @@ PAIRS = 2
 
 ROUND_GROUPS = 4
 BATCH_GROUPS = 8
+SCALE_DMA_GROUPS = 4
 LOADS_AHEAD = 3
 
 FLOPS = 2 * ROWS * K * H
@@ -101,15 +102,19 @@ def tile_evidentialhead_pa_k_kernel(tc, x, W1_words, W1_scales, b1, g, beta, out
             x_raw_of[i] = x_raw
 
         def load_scales(batch):
-            groups = slice(BATCH_GROUPS * batch, BATCH_GROUPS * (batch + 1))
-            for low in range(2):
-                for r in range(4):
-                    nc.sync.dma_start(
-                        out=w_planes_of[batch][32 * low + r : P : 64, :, :].bitcast(I32),
-                        in_=W1_scales[groups, 4 * low + r : 16 : 8, :]
-                        .bitcast(I32)
-                        .rearrange("g q n -> q g n"),
-                    )
+            for start in range(0, BATCH_GROUPS, SCALE_DMA_GROUPS):
+                here = slice(start, start + SCALE_DMA_GROUPS)
+                there = slice(
+                    BATCH_GROUPS * batch + start, BATCH_GROUPS * batch + start + SCALE_DMA_GROUPS
+                )
+                for low in range(2):
+                    for r in range(4):
+                        nc.sync.dma_start(
+                            out=w_planes_of[batch][32 * low + r : P : 64, here, :].bitcast(I32),
+                            in_=W1_scales[there, 4 * low + r : 16 : 8, :]
+                            .bitcast(I32)
+                            .rearrange("g q n -> q g n"),
+                        )
 
         def load_w(i):
             first, count = rounds[i]

@@ -27,26 +27,29 @@ COL_HALVES = H // N_PASS
 PAIRS = 2
 
 ROUND_GROUPS = 4
+FIRST_BATCH_GROUPS = 4
 BATCH_GROUPS = 8
-SCALE_DMA_GROUPS = 4
+W_DMA_GROUPS = 2
 LOADS_AHEAD = 3
+TAIL_ROUNDS = 2
 
 FLOPS = 2 * ROWS * K * H
 
 
-def cut_rounds():
-    rounds = []
+def cut_groups(shortest, longest):
+    pieces = []
     first = 0
     while first < GROUPS:
-        count = min(ROUND_GROUPS, max(1, first), max(1, (GROUPS - first) // 2))
-        rounds.append((first, count))
+        count = min(longest, max(shortest, first))
+        pieces.append((first, count))
         first += count
-    return rounds
+    return pieces
 
 
 def tile_evidentialhead_pa_k_kernel(tc, x, W1_words, W1_scales, b1, g, beta, out):
     nc = tc.nc
-    rounds = cut_rounds()
+    rounds = cut_groups(1, ROUND_GROUPS)
+    batches = cut_groups(FIRST_BATCH_GROUPS, BATCH_GROUPS)
     vectors = (b1, g, beta)
     x_by_tile = x.rearrange("(t b) k -> b t k", t=ROW_TILES)
 
@@ -54,17 +57,21 @@ def tile_evidentialhead_pa_k_kernel(tc, x, W1_words, W1_scales, b1, g, beta, out
         ctx.enter_context(tc.manual_schedule())
         keep = ctx.enter_context(tc.tile_pool(name="keep", bufs=1))
         x_pool = ctx.enter_context(tc.tile_pool(name="x_pool", bufs=LOADS_AHEAD + 1))
-        w_pool = ctx.enter_context(tc.tile_pool(name="w_pool", bufs=LOADS_AHEAD + 1))
+        w_pool = ctx.enter_context(
+            tc.tile_pool(name="w_pool", bufs=(LOADS_AHEAD + 1) * ROUND_GROUPS // W_DMA_GROUPS)
+        )
         stage = ctx.enter_context(tc.tile_pool(name="stage", bufs=2))
         codes = ctx.enter_context(tc.tile_pool(name="codes", bufs=2))
         sums_pool = ctx.enter_context(tc.psum_pool(name="sums_pool", bufs=1))
         banks = ctx.enter_context(tc.psum_pool(name="banks", bufs=4))
 
-        w_planes_of = {}
-        for batch in range(GROUPS // BATCH_GROUPS):
-            w_planes_of[batch] = keep.tile(
-                [P, BATCH_GROUPS, H], U8, name="w_planes_%d" % batch, align_bytes=64
-            )
+        batch_planes = []
+        w_plane_of = {}
+        for first, count in batches:
+            planes = keep.tile([P, count, H], U8, name="w_planes_%d" % first, align_bytes=64)
+            batch_planes.append(planes)
+            for j in range(count):
+                w_plane_of[first + j] = planes[:, j, :]
         ident = keep.tile([P, P], F32)
         ones = keep.tile([P, P], BF16)
         vec_rows = keep.tile([P, len(vectors), H], BF16)
@@ -76,9 +83,10 @@ def tile_evidentialhead_pa_k_kernel(tc, x, W1_words, W1_scales, b1, g, beta, out
                 acc[(t, c)] = sums_pool.tile([P, N_PASS], F32, name="acc_%d_%d" % (t, c))
 
         def zero_planes(batch):
-            nc.vector.memset(w_planes_of[batch][:].bitcast(I32), 0)
+            nc.vector.memset(batch_planes[batch][:].bitcast(I32), 0)
 
         zero_planes(0)
+        zero_planes(1)
         make_identity(nc, ident[:])
         nc.gpsimd.memset(ones[:], 1.0)
         nc.gpsimd.memset(vec_rows[:].bitcast(F32), 0.0)
@@ -102,30 +110,30 @@ def tile_evidentialhead_pa_k_kernel(tc, x, W1_words, W1_scales, b1, g, beta, out
             x_raw_of[i] = x_raw
 
         def load_scales(batch):
-            for start in range(0, BATCH_GROUPS, SCALE_DMA_GROUPS):
-                here = slice(start, start + SCALE_DMA_GROUPS)
-                there = slice(
-                    BATCH_GROUPS * batch + start, BATCH_GROUPS * batch + start + SCALE_DMA_GROUPS
-                )
-                for low in range(2):
-                    for r in range(4):
-                        nc.sync.dma_start(
-                            out=w_planes_of[batch][32 * low + r : P : 64, here, :].bitcast(I32),
-                            in_=W1_scales[there, 4 * low + r : 16 : 8, :]
-                            .bitcast(I32)
-                            .rearrange("g q n -> q g n"),
-                        )
+            first, count = batches[batch]
+            for low in range(2):
+                for r in range(4):
+                    nc.sync.dma_start(
+                        out=batch_planes[batch][32 * low + r : P : 64, :, :].bitcast(I32),
+                        in_=W1_scales[first : first + count, 4 * low + r : 16 : 8, :]
+                        .bitcast(I32)
+                        .rearrange("g q n -> q g n"),
+                    )
 
         def load_w(i):
             first, count = rounds[i]
-            if first % BATCH_GROUPS == 0:
-                load_scales(first // BATCH_GROUPS)
-            w_words = w_pool.tile([P, count, 2 * H], U8, tag="w_words", align_bytes=64)
-            nc.sync.dma_start(
-                out=w_words[:].bitcast(I32),
-                in_=W1_words[first : first + count].bitcast(I32).rearrange("g p n -> p g n"),
-            )
-            w_words_of[i] = w_words
+            for batch in range(len(batches)):
+                if batches[batch][0] == first:
+                    load_scales(batch)
+            for start in range(first, first + count, W_DMA_GROUPS):
+                stop = min(start + W_DMA_GROUPS, first + count)
+                w_words = w_pool.tile([P, stop - start, 2 * H], U8, tag="w_words", align_bytes=64)
+                nc.sync.dma_start(
+                    out=w_words[:].bitcast(I32),
+                    in_=W1_words[start:stop].bitcast(I32).rearrange("g p n -> p g n"),
+                )
+                for group in range(start, stop):
+                    w_words_of[group] = w_words[:, group - start, :]
 
         def sort_words(i):
             count = rounds[i][1]
@@ -170,26 +178,17 @@ def tile_evidentialhead_pa_k_kernel(tc, x, W1_words, W1_scales, b1, g, beta, out
             x_codes_of[i] = x_codes
             x_planes_of[i] = x_planes
 
-        def multiply(i):
-            first, count = rounds[i]
-            for j in range(count):
-                group = first + j
-                w_planes = w_planes_of[group // BATCH_GROUPS]
-                for t in range(ROW_TILES):
-                    for c in range(COL_HALVES):
-                        nc.tensor.matmul_mx(
-                            out=acc[(t, c)][:],
-                            lhsT=x_codes_of[i][:, j, t, :].bitcast(FP8X4),
-                            lhsT_scale=x_planes_of[i][:, j, t, :],
-                            rhs=w_words_of[i][
-                                :, j, 2 * N_PASS * c : 2 * N_PASS * (c + 1)
-                            ].bitcast(FP4X4),
-                            rhs_scale=w_planes[
-                                :, group % BATCH_GROUPS, N_PASS * c : N_PASS * (c + 1)
-                            ],
-                            start=(group == 0),
-                            stop=(group == GROUPS - 1),
-                        )
+        def one_pass(i, j, t, c):
+            group = rounds[i][0] + j
+            nc.tensor.matmul_mx(
+                out=acc[(t, c)][:],
+                lhsT=x_codes_of[i][:, j, t, :].bitcast(FP8X4),
+                lhsT_scale=x_planes_of[i][:, j, t, :],
+                rhs=w_words_of[group][:, 2 * N_PASS * c : 2 * N_PASS * (c + 1)].bitcast(FP4X4),
+                rhs_scale=w_plane_of[group][:, N_PASS * c : N_PASS * (c + 1)],
+                start=(group == 0),
+                stop=(group == GROUPS - 1),
+            )
 
         def spread_vector(j):
             for c in range(COL_HALVES):
@@ -200,6 +199,7 @@ def tile_evidentialhead_pa_k_kernel(tc, x, W1_words, W1_scales, b1, g, beta, out
                 )
                 nc.scalar.copy(out=spread[:, j, cols], in_=bank[:])
 
+        first_tail_round = len(rounds) - TAIL_ROUNDS
         load_x(0)
         for i in range(LOADS_AHEAD):
             load_x(i + 1)
@@ -214,54 +214,65 @@ def tile_evidentialhead_pa_k_kernel(tc, x, W1_words, W1_scales, b1, g, beta, out
             if i + 1 < len(rounds):
                 sort_words(i + 1)
             quantise(i)
-            if i + 1 < GROUPS // BATCH_GROUPS:
-                zero_planes(i + 1)
+            if i + 2 < len(batches):
+                zero_planes(i + 2)
             if i + 1 < len(rounds):
                 turn(i + 1)
-            multiply(i)
+            for j in range(rounds[i][1]):
+                for t in range(ROW_TILES if i < first_tail_round else 1):
+                    for c in range(COL_HALVES):
+                        one_pass(i, j, t, c)
             if i < len(vectors):
                 spread_vector(i)
 
+        for c in range(COL_HALVES):
+            for i in range(first_tail_round, len(rounds)):
+                for j in range(rounds[i][1]):
+                    one_pass(i, j, ROW_TILES - 1, c)
+
         h_of = {}
         row_sums_of = {}
+        neg_mean_of = {}
         centred_of = {}
         square_sum_of = {}
         for t in range(ROW_TILES):
-            h = keep.tile([P, H], F32, name="h_%d" % t)
-            row_sums = keep.tile([P, COL_HALVES], F32, name="row_sums_%d" % t)
-            for c in range(COL_HALVES):
-                cols = slice(N_PASS * c, N_PASS * (c + 1))
-                nc.vector.tensor_tensor(
-                    out=h[:, cols], in0=acc[(t, c)][:], in1=spread[:, 0, cols], op=ALU.add
-                )
-                nc.scalar.activation(
-                    out=h[:, cols], in_=h[:, cols], func=ACT.Silu,
-                    accum_out=row_sums[:, c : c + 1],
-                )
-            h_of[t] = h
-            row_sums_of[t] = row_sums
+            h_of[t] = keep.tile([P, H], F32, name="h_%d" % t)
+            row_sums_of[t] = keep.tile([P, COL_HALVES], F32, name="row_sums_%d" % t)
+            neg_mean_of[t] = keep.tile([P, COL_HALVES], F32, name="neg_mean_%d" % t)
 
-        for t in range(ROW_TILES):
-            neg_mean = keep.tile([P, 1], F32, name="neg_mean_%d" % t)
-            nc.gpsimd.tensor_scalar(
-                out=neg_mean[:], in0=row_sums_of[t][:, 0:1], scalar1=row_sums_of[t][:, 1:2],
-                scalar2=-1.0 / H, op0=ALU.add, op1=ALU.mult,
+        def activate(t, c):
+            cols = slice(N_PASS * c, N_PASS * (c + 1))
+            h = h_of[t]
+            nc.vector.tensor_tensor(
+                out=h[:, cols], in0=acc[(t, c)][:], in1=spread[:, 0, cols], op=ALU.add
             )
+            nc.scalar.activation(
+                out=h[:, cols], in_=h[:, cols], func=ACT.Silu,
+                accum_out=row_sums_of[t][:, c : c + 1],
+            )
+            nc.scalar.activation(
+                out=neg_mean_of[t][:, c : c + 1], in_=row_sums_of[t][:, c : c + 1],
+                func=ACT.Identity, scale=-1.0 / H,
+                bias=(neg_mean_of[t][:, c - 1 : c] if c > 0 else 0.0),
+            )
+
+        def centre(t):
+            neg_mean = neg_mean_of[t][:, COL_HALVES - 1 : COL_HALVES]
             squares = keep.tile([P, H], F32, name="squares_%d" % t)
             square_sum = keep.tile([P, 1], F32, name="square_sum_%d" % t)
             nc.scalar.activation(
-                out=squares[:], in_=h_of[t][:], func=ACT.Square, bias=neg_mean[:, 0:1],
+                out=squares[:], in_=h_of[t][:], func=ACT.Square, bias=neg_mean,
                 accum_out=square_sum[:, 0:1],
             )
             centred = keep.tile([P, H], F32, name="centred_%d" % t)
             nc.vector.scalar_tensor_tensor(
-                out=centred[:], in0=h_of[t][:], scalar=neg_mean[:, 0:1], in1=spread[:, 1, :],
+                out=centred[:], in0=h_of[t][:], scalar=neg_mean, in1=spread[:, 1, :],
                 op0=ALU.add, op1=ALU.mult,
             )
             square_sum_of[t] = square_sum
             centred_of[t] = centred
 
-        for t in range(ROW_TILES):
+        def normalise(t):
             var_eps = keep.tile([P, 1], F32, name="var_eps_%d" % t)
             nc.gpsimd.tensor_scalar(
                 out=var_eps[:], in0=square_sum_of[t][:], scalar1=1.0 / H, scalar2=EPS_LN,
@@ -278,3 +289,12 @@ def tile_evidentialhead_pa_k_kernel(tc, x, W1_words, W1_scales, b1, g, beta, out
                 nc.sync.dma_start(
                     out=out[P * t : P * (t + 1), cols], in_=centred_of[t][:, cols]
                 )
+
+        activate(0, 0)
+        activate(0, 1)
+        centre(0)
+        activate(1, 0)
+        activate(1, 1)
+        normalise(0)
+        centre(1)
+        normalise(1)

@@ -31,6 +31,7 @@ FIRST_BATCH_GROUPS = 4
 BATCH_GROUPS = 8
 W_DMA_GROUPS = 2
 LOADS_AHEAD = 3
+RAMP_GROUPS = 12
 TAIL_ROUNDS = 2
 
 FLOPS = 2 * ROWS * K * H
@@ -94,7 +95,7 @@ def tile_evidentialhead_pa_k_kernel(tc, x, W1_words, W1_scales, b1, g, beta, out
         for j, vector in enumerate(vectors):
             nc.scalar.dma_start(out=vec_rows[0:1, j, :], in_=vector.unsqueeze(0))
 
-        x_raw_of = {}
+        x_group_of = {}
         x_sorted_of = {}
         grouped_of = {}
         w_words_of = {}
@@ -103,11 +104,21 @@ def tile_evidentialhead_pa_k_kernel(tc, x, W1_words, W1_scales, b1, g, beta, out
 
         def load_x(i):
             first, count = rounds[i]
-            x_raw = x_pool.tile([P, ROW_TILES, count * K_PASS], BF16, tag="x_raw")
-            nc.sync.dma_start(
-                out=x_raw[:], in_=x_by_tile[:, :, first * K_PASS : (first + count) * K_PASS]
-            )
-            x_raw_of[i] = x_raw
+            if first < RAMP_GROUPS:
+                x_raw = x_pool.tile([P, count, ROW_TILES, K_PASS], BF16, tag="x_raw")
+                for j in range(count):
+                    group = first + j
+                    nc.sync.dma_start(
+                        out=x_raw[:, j, :, :], in_=x_by_tile[:, :, group * K_PASS : (group + 1) * K_PASS]
+                    )
+                    x_group_of[group] = x_raw[:, j, :, :]
+            else:
+                x_raw = x_pool.tile([P, ROW_TILES, count * K_PASS], BF16, tag="x_raw")
+                nc.sync.dma_start(
+                    out=x_raw[:], in_=x_by_tile[:, :, first * K_PASS : (first + count) * K_PASS]
+                )
+                for j in range(count):
+                    x_group_of[first + j] = x_raw[:, :, j * K_PASS : (j + 1) * K_PASS]
 
         def load_scales(batch):
             first, count = batches[batch]
@@ -128,22 +139,23 @@ def tile_evidentialhead_pa_k_kernel(tc, x, W1_words, W1_scales, b1, g, beta, out
             for start in range(first, first + count, W_DMA_GROUPS):
                 stop = min(start + W_DMA_GROUPS, first + count)
                 w_words = w_pool.tile([P, stop - start, 2 * H], U8, tag="w_words", align_bytes=64)
-                nc.sync.dma_start(
-                    out=w_words[:].bitcast(I32),
-                    in_=W1_words[start:stop].bitcast(I32).rearrange("g p n -> p g n"),
-                )
+                step = 1 if first < RAMP_GROUPS else stop - start
+                for low in range(start, stop, step):
+                    nc.sync.dma_start(
+                        out=w_words[:, low - start : low - start + step, :].bitcast(I32),
+                        in_=W1_words[low : low + step].bitcast(I32).rearrange("g p n -> p g n"),
+                    )
                 for group in range(start, stop):
                     w_words_of[group] = w_words[:, group - start, :]
 
         def sort_words(i):
-            count = rounds[i][1]
-            x_sorted = stage.tile([P, ROW_TILES, count, PAIRS, P], F32, tag="x_sorted")
-            nc.vector.tensor_copy(
-                out=x_sorted[:].rearrange("b t g u p -> b (t g) u p"),
-                in_=x_raw_of[i][:]
-                .bitcast(F32)
-                .rearrange("b t (g p u) -> b (t g) u p", p=P, u=PAIRS),
-            )
+            first, count = rounds[i]
+            x_sorted = stage.tile([P, count, ROW_TILES, PAIRS, P], F32, tag="x_sorted")
+            for j in range(count):
+                nc.vector.tensor_copy(
+                    out=x_sorted[:, j, :, :, :],
+                    in_=x_group_of[first + j].bitcast(F32).rearrange("b t (p u) -> b t u p", u=PAIRS),
+                )
             x_sorted_of[i] = x_sorted
 
         def turn(i):
@@ -159,7 +171,7 @@ def tile_evidentialhead_pa_k_kernel(tc, x, W1_words, W1_scales, b1, g, beta, out
                 for t in range(ROW_TILES):
                     for u in range(PAIRS):
                         nc.tensor.transpose(
-                            bank[:, t, u, :], x_sorted_of[i][:, t, j, u, :], ident[:]
+                            bank[:, t, u, :], x_sorted_of[i][:, j, t, u, :], ident[:]
                         )
                 nc.scalar.copy(
                     out=grouped_words[:, j], in_=bank[:].rearrange("p t u r -> p t r u")
@@ -167,14 +179,17 @@ def tile_evidentialhead_pa_k_kernel(tc, x, W1_words, W1_scales, b1, g, beta, out
             grouped_of[i] = grouped
 
         def quantise(i):
-            count = rounds[i][1]
+            first, count = rounds[i]
             x_codes = codes.tile([P, count, ROW_TILES, P], U32, tag="x_codes", align_bytes=64)
             x_planes = codes.tile([P, count, ROW_TILES, P], U8, tag="x_planes", align_bytes=64)
-            nc.vector.quantize_mx(
-                out=x_codes[:].rearrange("p g t r -> p (g t r)").bitcast(FP8X4),
-                scales=x_planes[:].rearrange("p g t r -> p (g t r)"),
-                in_=grouped_of[i][:],
-            )
+            step = 1 if first < RAMP_GROUPS else count
+            width = ROW_TILES * P * 4
+            for j in range(0, count, step):
+                nc.vector.quantize_mx(
+                    out=x_codes[:, j : j + step, :, :].rearrange("p g t r -> p (g t r)").bitcast(FP8X4),
+                    scales=x_planes[:, j : j + step, :, :].rearrange("p g t r -> p (g t r)"),
+                    in_=grouped_of[i][:, j * width : (j + step) * width],
+                )
             x_codes_of[i] = x_codes
             x_planes_of[i] = x_planes
 

@@ -92,8 +92,6 @@ def tile_evidentialhead_pa_k_kernel(tc, x, W1_words, W1_scales, b1, g, beta, out
         nc.gpsimd.memset(ones[:], 1.0)
         nc.gpsimd.memset(vec_rows[:].bitcast(F32), 0.0)
         nc.gpsimd.memset(neg_half[:], -0.5)
-        for j, vector in enumerate(vectors):
-            nc.scalar.dma_start(out=vec_rows[0:1, j, :], in_=vector.unsqueeze(0))
 
         x_group_of = {}
         x_sorted_of = {}
@@ -122,11 +120,12 @@ def tile_evidentialhead_pa_k_kernel(tc, x, W1_words, W1_scales, b1, g, beta, out
 
         def load_scales(batch):
             first, count = batches[batch]
-            for low in range(2):
+            pitch = 32 if batch == 0 else 64
+            for low in range(pitch // 32):
                 for r in range(4):
                     nc.sync.dma_start(
-                        out=batch_planes[batch][32 * low + r : P : 64, :, :].bitcast(I32),
-                        in_=W1_scales[first : first + count, 4 * low + r : 16 : 8, :]
+                        out=batch_planes[batch][32 * low + r : P : pitch, :, :].bitcast(I32),
+                        in_=W1_scales[first : first + count, 4 * low + r : 16 : pitch // 8, :]
                         .bitcast(I32)
                         .rearrange("g q n -> q g n"),
                     )
@@ -219,6 +218,9 @@ def tile_evidentialhead_pa_k_kernel(tc, x, W1_words, W1_scales, b1, g, beta, out
         for i in range(LOADS_AHEAD):
             load_x(i + 1)
             load_w(i)
+            if i == 1:
+                for j, vector in enumerate(vectors):
+                    nc.sync.dma_start(out=vec_rows[0:1, j, :], in_=vector.unsqueeze(0))
         sort_words(0)
         turn(0)
         for i in range(len(rounds)):

from contextlib import ExitStack

import concourse.mybir as mybir
from concourse.masks import make_identity

F32 = mybir.dt.float32
BF16 = mybir.dt.bfloat16
I32 = mybir.dt.int32
U32 = mybir.dt.uint32
U8 = mybir.dt.uint8
FP8X4 = mybir.dt.float8_e4m3fn_x4
FP4X4 = mybir.dt.float4_e2m1fn_x4
ALU = mybir.AluOpType
ACT = mybir.ActivationFunctionType

P = 128
ROWS = 256
K = 16384
H = 1024
EPS_LN = 1e-5

K_PASS = 4 * P
GROUPS = K // K_PASS
ROW_TILES = ROWS // P
N_PASS = 512
COL_HALVES = H // N_PASS
PAIRS = 2

ROUND_GROUPS = 4
FIRST_BATCH_GROUPS = 4
BATCH_GROUPS = 8
W_DMA_GROUPS = 2
LOADS_AHEAD = 3
RAMP_GROUPS = 12
TAIL_ROUNDS = 2

FLOPS = 2 * ROWS * K * H


def cut_groups(shortest, longest):
    pieces = []
    first = 0
    while first < GROUPS:
        count = min(longest, max(shortest, first))
        pieces.append((first, count))
        first += count
    return pieces


def tile_evidentialhead_pa_k_kernel(tc, x, W1_words, W1_scales, b1, g, beta, out):
    nc = tc.nc
    rounds = cut_groups(1, ROUND_GROUPS)
    batches = cut_groups(FIRST_BATCH_GROUPS, BATCH_GROUPS)
    vectors = (b1, g, beta)
    x_by_tile = x.rearrange("(t b) k -> b t k", t=ROW_TILES)

    with ExitStack() as ctx:
        ctx.enter_context(tc.manual_schedule())
        keep = ctx.enter_context(tc.tile_pool(name="keep", bufs=1))
        x_pool = ctx.enter_context(tc.tile_pool(name="x_pool", bufs=LOADS_AHEAD + 1))
        w_pool = ctx.enter_context(
            tc.tile_pool(name="w_pool", bufs=(LOADS_AHEAD + 1) * ROUND_GROUPS // W_DMA_GROUPS)
        )
        stage = ctx.enter_context(tc.tile_pool(name="stage", bufs=2))
        codes = ctx.enter_context(tc.tile_pool(name="codes", bufs=2))
        sums_pool = ctx.enter_context(tc.psum_pool(name="sums_pool", bufs=1))
        banks = ctx.enter_context(tc.psum_pool(name="banks", bufs=4))

        batch_planes = []
        w_plane_of = {}
        for first, count in batches:
            planes = keep.tile([P, count, H], U8, name="w_planes_%d" % first, align_bytes=64)
            batch_planes.append(planes)
            for j in range(count):
                w_plane_of[first + j] = planes[:, j, :]
        ident = keep.tile([P, P], F32)
        ones = keep.tile([P, P], BF16)
        vec_rows = keep.tile([P, len(vectors), H], BF16)
        spread = keep.tile([P, len(vectors), H], F32)
        neg_half = keep.tile([P, 1], F32)
        acc = {}
        for t in range(ROW_TILES):
            for c in range(COL_HALVES):
                acc[(t, c)] = sums_pool.tile([P, N_PASS], F32, name="acc_%d_%d" % (t, c))

        def zero_planes(batch):
            nc.vector.memset(batch_planes[batch][:].bitcast(I32), 0)

        zero_planes(0)
        zero_planes(1)
        make_identity(nc, ident[:])
        nc.gpsimd.memset(ones[:], 1.0)
        nc.gpsimd.memset(vec_rows[:].bitcast(F32), 0.0)
        nc.gpsimd.memset(neg_half[:], -0.5)

        x_group_of = {}
        x_sorted_of = {}
        grouped_of = {}
        w_words_of = {}
        x_codes_of = {}
        x_planes_of = {}

        def load_x(i):
            first, count = rounds[i]
            if first < RAMP_GROUPS:
                x_raw = x_pool.tile([P, count, ROW_TILES, K_PASS], BF16, tag="x_raw")
                for j in range(count):
                    group = first + j
                    nc.sync.dma_start(
                        out=x_raw[:, j, :, :], in_=x_by_tile[:, :, group * K_PASS : (group + 1) * K_PASS]
                    )
                    x_group_of[group] = x_raw[:, j, :, :]
            else:
                x_raw = x_pool.tile([P, ROW_TILES, count * K_PASS], BF16, tag="x_raw")
                nc.sync.dma_start(
                    out=x_raw[:], in_=x_by_tile[:, :, first * K_PASS : (first + count) * K_PASS]
                )
                for j in range(count):
                    x_group_of[first + j] = x_raw[:, :, j * K_PASS : (j + 1) * K_PASS]

        def load_scales(batch):
            first, count = batches[batch]
            pitch = 32 if batch == 0 else 64
            for low in range(pitch // 32):
                for r in range(4):
                    nc.sync.dma_start(
                        out=batch_planes[batch][32 * low + r : P : pitch, :, :].bitcast(I32),
                        in_=W1_scales[first : first + count, 4 * low + r : 16 : pitch // 8, :]
                        .bitcast(I32)
                        .rearrange("g q n -> q g n"),
                    )

        def load_w(i):
            first, count = rounds[i]
            for batch in range(len(batches)):
                if batches[batch][0] == first:
                    load_scales(batch)
            for start in range(first, first + count, W_DMA_GROUPS):
                stop = min(start + W_DMA_GROUPS, first + count)
                w_words = w_pool.tile([P, stop - start, 2 * H], U8, tag="w_words", align_bytes=64)
                step = 1 if first < RAMP_GROUPS else stop - start
                for low in range(start, stop, step):
                    nc.sync.dma_start(
                        out=w_words[:, low - start : low - start + step, :].bitcast(I32),
                        in_=W1_words[low : low + step].bitcast(I32).rearrange("g p n -> p g n"),
                    )
                for group in range(start, stop):
                    w_words_of[group] = w_words[:, group - start, :]

        def sort_words(i):
            first, count = rounds[i]
            x_sorted = stage.tile([P, count, ROW_TILES, PAIRS, P], F32, tag="x_sorted")
            for j in range(count):
                nc.vector.tensor_copy(
                    out=x_sorted[:, j, :, :, :],
                    in_=x_group_of[first + j].bitcast(F32).rearrange("b t (p u) -> b t u p", u=PAIRS),
                )
            x_sorted_of[i] = x_sorted

        def turn(i):
            count = rounds[i][1]
            grouped = stage.tile(
                [P, count * ROW_TILES * P * 4], BF16, tag="grouped", align_bytes=64
            )
            grouped_words = grouped[:].bitcast(F32).rearrange(
                "p (g t r u) -> p g t r u", g=count, t=ROW_TILES, u=PAIRS
            )
            for j in range(count):
                bank = banks.tile([P, ROW_TILES, PAIRS, P], F32, tag="bank")
                for t in range(ROW_TILES):
                    for u in range(PAIRS):
                        nc.tensor.transpose(
                            bank[:, t, u, :], x_sorted_of[i][:, j, t, u, :], ident[:]
                        )
                nc.scalar.copy(
                    out=grouped_words[:, j], in_=bank[:].rearrange("p t u r -> p t r u")
                )
            grouped_of[i] = grouped

        def quantise(i):
            first, count = rounds[i]
            x_codes = codes.tile([P, count, ROW_TILES, P], U32, tag="x_codes", align_bytes=64)
            x_planes = codes.tile([P, count, ROW_TILES, P], U8, tag="x_planes", align_bytes=64)
            step = 1 if first < RAMP_GROUPS else count
            width = ROW_TILES * P * 4
            for j in range(0, count, step):
                nc.vector.quantize_mx(
                    out=x_codes[:, j : j + step, :, :].rearrange("p g t r -> p (g t r)").bitcast(FP8X4),
                    scales=x_planes[:, j : j + step, :, :].rearrange("p g t r -> p (g t r)"),
                    in_=grouped_of[i][:, j * width : (j + step) * width],
                )
            x_codes_of[i] = x_codes
            x_planes_of[i] = x_planes

        def one_pass(i, j, t, c):
            group = rounds[i][0] + j
            nc.tensor.matmul_mx(
                out=acc[(t, c)][:],
                lhsT=x_codes_of[i][:, j, t, :].bitcast(FP8X4),
                lhsT_scale=x_planes_of[i][:, j, t, :],
                rhs=w_words_of[group][:, 2 * N_PASS * c : 2 * N_PASS * (c + 1)].bitcast(FP4X4),
                rhs_scale=w_plane_of[group][:, N_PASS * c : N_PASS * (c + 1)],
                start=(group == 0),
                stop=(group == GROUPS - 1),
            )

        def spread_vector(j):
            for c in range(COL_HALVES):
                cols = slice(N_PASS * c, N_PASS * (c + 1))
                bank = banks.tile([P, N_PASS], F32, tag="bank")
                nc.tensor.matmul(
                    out=bank[:], lhsT=ones[:], rhs=vec_rows[:, j, cols], start=True, stop=True
                )
                nc.scalar.copy(out=spread[:, j, cols], in_=bank[:])

        first_tail_round = len(rounds) - TAIL_ROUNDS
        load_x(0)
        for i in range(LOADS_AHEAD):
            load_x(i + 1)
            load_w(i)
            if i == 1:
                for j, vector in enumerate(vectors):
                    nc.sync.dma_start(out=vec_rows[0:1, j, :], in_=vector.unsqueeze(0))
        sort_words(0)
        turn(0)
        for i in range(len(rounds)):
            if i + LOADS_AHEAD + 1 < len(rounds):
                load_x(i + LOADS_AHEAD + 1)
            if i + LOADS_AHEAD < len(rounds):
                load_w(i + LOADS_AHEAD)
            if i + 1 < len(rounds):
                sort_words(i + 1)
            quantise(i)
            if i + 2 < len(batches):
                zero_planes(i + 2)
            if i + 1 < len(rounds):
                turn(i + 1)
            for j in range(rounds[i][1]):
                for t in range(ROW_TILES if i < first_tail_round else 1):
                    for c in range(COL_HALVES):
                        one_pass(i, j, t, c)
            if i < len(vectors):
                spread_vector(i)

        for c in range(COL_HALVES):
            for i in range(first_tail_round, len(rounds)):
                for j in range(rounds[i][1]):
                    one_pass(i, j, ROW_TILES - 1, c)

        h_of = {}
        row_sums_of = {}
        neg_mean_of = {}
        centred_of = {}
        square_sum_of = {}
        for t in range(ROW_TILES):
            h_of[t] = keep.tile([P, H], F32, name="h_%d" % t)
            row_sums_of[t] = keep.tile([P, COL_HALVES], F32, name="row_sums_%d" % t)
            neg_mean_of[t] = keep.tile([P, COL_HALVES], F32, name="neg_mean_%d" % t)

        def activate(t, c):
            cols = slice(N_PASS * c, N_PASS * (c + 1))
            h = h_of[t]
            nc.vector.tensor_tensor(
                out=h[:, cols], in0=acc[(t, c)][:], in1=spread[:, 0, cols], op=ALU.add
            )
            nc.scalar.activation(
                out=h[:, cols], in_=h[:, cols], func=ACT.Silu,
                accum_out=row_sums_of[t][:, c : c + 1],
            )
            nc.scalar.activation(
                out=neg_mean_of[t][:, c : c + 1], in_=row_sums_of[t][:, c : c + 1],
                func=ACT.Identity, scale=-1.0 / H,
                bias=(neg_mean_of[t][:, c - 1 : c] if c > 0 else 0.0),
            )

        def centre(t):
            neg_mean = neg_mean_of[t][:, COL_HALVES - 1 : COL_HALVES]
            squares = keep.tile([P, H], F32, name="squares_%d" % t)
            square_sum = keep.tile([P, 1], F32, name="square_sum_%d" % t)
            nc.scalar.activation(
                out=squares[:], in_=h_of[t][:], func=ACT.Square, bias=neg_mean,
                accum_out=square_sum[:, 0:1],
            )
            centred = keep.tile([P, H], F32, name="centred_%d" % t)
            nc.vector.scalar_tensor_tensor(
                out=centred[:], in0=h_of[t][:], scalar=neg_mean, in1=spread[:, 1, :],
                op0=ALU.add, op1=ALU.mult,
            )
            square_sum_of[t] = square_sum
            centred_of[t] = centred

        def normalise(t):
            var_eps = keep.tile([P, 1], F32, name="var_eps_%d" % t)
            nc.gpsimd.tensor_scalar(
                out=var_eps[:], in0=square_sum_of[t][:], scalar1=1.0 / H, scalar2=EPS_LN,
                op0=ALU.mult, op1=ALU.add,
            )
            rstd = keep.tile([P, 1], F32, name="rstd_%d" % t)
            nc.gpsimd.tensor_tensor(out=rstd[:], in0=var_eps[:], in1=neg_half[:], op=ALU.pow)
            for c in range(COL_HALVES):
                cols = slice(N_PASS * c, N_PASS * (c + 1))
                nc.vector.scalar_tensor_tensor(
                    out=centred_of[t][:, cols], in0=centred_of[t][:, cols], scalar=rstd[:, 0:1],
                    in1=spread[:, 2, cols], op0=ALU.mult, op1=ALU.add,
                )
                nc.sync.dma_start(
                    out=out[P * t : P * (t + 1), cols], in_=centred_of[t][:, cols]
                )

        activate(0, 0)
        activate(0, 1)
        centre(0)
        activate(1, 0)
        activate(1, 1)
        normalise(0)
        centre(1)
        normalise(1)
